import numpy as np
import ml_dtypes


def mxq(x, axis, fmt="e4m3"):
    dtype, down = {"e4m3": (ml_dtypes.float8_e4m3fn, 7), "e5m2": (ml_dtypes.float8_e5m2, 14)}[fmt]
    v = np.moveaxis(np.asarray(x, np.float32).astype(ml_dtypes.bfloat16).astype(np.float64), axis, -1)
    blocks = v.reshape(v.shape[:-1] + (-1, 32))
    amax = np.abs(blocks).max(-1, keepdims=True)
    byte = np.maximum(np.where(amax > 0, np.frexp(amax)[1] - 1 + 127, 0) - down, 1)
    scale = np.exp2(byte - 127.0)
    codes = (blocks / scale).astype(np.float32).astype(dtype).astype(np.float64)
    return np.moveaxis((codes * scale).reshape(v.shape), -1, axis)


WIDE = False


def mx_kscale(k):
    if not WIDE:
        return np.ones(k)
    levels = np.array([10, -10, 5, -5, 0])
    if k % 512:
        return np.exp2(np.random.permutation(np.resize(levels, k // 32))).repeat(32)
    a = np.empty((k // 512, 16))
    for p in range(k // 512):
        a[p, :8] = np.random.permutation(np.resize(levels, 8))
        for g in range(8):
            far = levels[np.abs(levels - a[p, g]) >= 10]
            a[p, g + 8] = far[np.random.randint(len(far))]
    return np.exp2(a.ravel()).repeat(32)


BF16 = ml_dtypes.bfloat16


def bf(x):
    return np.asarray(x, np.float32).astype(BF16)


def f64(x):
    return np.asarray(x).astype(np.float64)


B, EN_MID, DE_MID = 1024, 1024, 2048
K1 = EN_MID // 2
K2 = DE_MID // 2


def setup_inputs():
    s = mx_kscale(B)
    u = mx_kscale(DE_MID)[:K2]
    uu = np.concatenate([u, u])
    in0 = bf(np.random.standard_normal((B, K1, 2)).reshape(B, EN_MID))
    W0 = bf(np.random.standard_normal((DE_MID, K1)) / np.sqrt(K1))
    bias = bf(np.random.standard_normal(DE_MID) * 0.25)
    g = bf(np.random.standard_normal((B, K2, 2)) * np.exp2(np.random.randint(-6, 1, (B, 1, 1)))
           / s[:, None, None] * u[None, :, None]).reshape(B, DE_MID, 1)
    z = f64(in0).reshape(B, K1, 2)[:, :, 1] @ f64(W0).T + f64(bias)
    return {"in_data": bf(f64(in0) * s[:, None]), "W": bf(f64(W0) / uu[:, None]), "bias": bias,
            "z": np.asarray(z, np.float32), "grad_out": g}


def reference(in_data, W, bias, z, grad_out):
    n = in_data.shape[0]
    x = f64(in_data).reshape(n, K1, 2)[:, :, 1]
    gr = f64(grad_out).reshape(n, K2, 2)[:, :, 0]
    dact = np.concatenate([gr, -gr], axis=1)
    dz = np.where(f64(z) > 0.0, dact, 0.0)
    dx = mxq(dz, 1, "e5m2") @ mxq(f64(W), 0, "e4m3")
    dW = mxq(dz, 0, "e5m2").T @ mxq(x, 0, "e4m3")
    g_in = np.stack([np.zeros_like(dx), dx], axis=2).reshape(n, EN_MID)
    return g_in, dW

@@ -1,0 +1,249 @@
+from contextlib import ExitStack
+
+import concourse.mybir as mybir
+from concourse.masks import make_identity
+
+B, EN_MID, DE_MID = 1024, 1024, 2048
+K1 = EN_MID // 2
+K2 = DE_MID // 2
+
+FLOPS = 2 * 2 * B * DE_MID * K1
+BYTES = B * K1 * 2 + DE_MID * K1 * 2 + B * DE_MID * 4 + B * K2 * 2 + B * EN_MID * 4 + DE_MID * K1 * 4
+
+F32 = mybir.dt.float32
+BF16 = mybir.dt.bfloat16
+U32 = mybir.dt.uint32
+U8 = mybir.dt.uint8
+E4X4 = mybir.dt.float8_e4m3fn_x4
+E5X4 = mybir.dt.float8_e5m2_x4
+ALU = mybir.AluOpType
+
+P = 128
+RAW8 = 9
+RAW4 = 6
+
+ORDER = [
+    ("LW", 0, 0, ""), ("LG", 0, 0, ""), ("Lz", 0, 0, ""), ("LW", 1, 0, ""),
+    ("LG", 1, 0, ""), ("Lz", 1, 0, ""), ("LW", 2, 0, ""), ("LW", 3, 0, ""),
+    ("Lg", 1, 0, ""), ("Lz", 2, 0, ""), ("Lz", 3, 0, ""), ("Lg", 2, 0, ""),
+    ("Lz", 4, 0, ""), ("Lz", 5, 0, ""), ("Lg", 3, 0, ""), ("IW", 0, 0, "S"),
+    ("QW", 0, 0, ""), ("D", 0, 0, ""), ("IW", 1, 0, "V"), ("Lz", 6, 0, ""),
+    ("T", 0, 0, ""), ("T", 0, 1, ""), ("C", 0, 0, "S"), ("QW", 1, 0, ""),
+    ("C", 0, 1, "S"), ("Q", 0, 0, ""), ("D", 1, 0, ""), ("IW", 2, 0, "V"),
+    ("Lz", 7, 0, ""), ("T", 1, 0, ""), ("T", 1, 1, ""), ("C", 1, 0, "S"),
+    ("QW", 2, 0, ""), ("C", 1, 1, "S"), ("IW", 3, 0, "V"), ("QW", 3, 0, ""),
+    ("Q", 1, 0, ""), ("M", 0, 0, ""), ("D", 2, 0, ""), ("M", 1, 0, ""),
+    ("E", 0, 0, "S"), ("D", 3, 0, ""), ("T", 2, 0, ""), ("E", 1, 0, "S"),
+    ("T", 2, 1, ""), ("C", 2, 0, "S"), ("S0", 0, 0, ""), ("I", 0, 2, "V"),
+    ("Lx", 0, 0, ""), ("T", 3, 0, ""), ("C", 2, 1, "S"), ("Lx", 1, 0, ""),
+    ("T", 3, 1, ""), ("I", 0, 0, "S"), ("Q", 2, 0, ""), ("D", 4, 0, ""),
+    ("M", 2, 0, ""), ("C", 3, 0, "S"), ("C", 3, 1, "S"), ("D", 5, 0, ""),
+    ("T", 4, 0, ""), ("E", 2, 0, "S"), ("T", 4, 1, ""), ("C", 4, 0, "S"),
+    ("Q", 3, 0, ""), ("C", 4, 1, "S"), ("T", 5, 0, ""), ("QA", 0, 0, ""),
+    ("T", 5, 1, ""), ("I", 0, 1, "S"), ("Q", 4, 0, ""), ("M", 3, 0, ""),
+    ("D", 6, 0, ""), ("M", 4, 0, ""), ("C", 5, 0, "S"), ("C", 5, 1, "S"),
+    ("D", 7, 0, ""), ("T", 6, 0, ""), ("E", 3, 0, "S"), ("T", 6, 1, ""),
+    ("C", 6, 0, "S"), ("S0", 1, 0, ""), ("Q", 5, 0, ""), ("T", 7, 0, ""),
+    ("C", 6, 1, "S"), ("QA", 0, 1, ""), ("T", 7, 1, ""), ("E", 4, 0, "S"),
+    ("Q", 6, 0, ""), ("M", 5, 0, ""), ("QA", 0, 2, ""), ("C", 7, 0, "S"),
+    ("IX", 0, 0, "V"), ("M", 6, 0, ""), ("I", 1, 0, "S"), ("QX", 0, 0, ""),
+    ("IX", 1, 0, "V"), ("C", 7, 1, "S"), ("QX", 1, 0, ""), ("E", 5, 0, "S"),
+    ("QA", 1, 0, ""), ("I", 1, 1, "V"), ("MA", 0, 0, ""), ("E", 6, 0, "S"),
+    ("MA", 1, 0, ""), ("S0", 2, 0, ""), ("MA", 2, 0, ""), ("EA", 0, 0, "V"),
+    ("MA", 3, 0, ""), ("QA", 1, 1, ""), ("EA", 1, 0, "S"), ("I", 1, 2, "V"),
+    ("MA", 4, 0, ""), ("EA", 2, 0, "S"), ("S1", 0, 2, ""), ("MA", 5, 0, ""),
+    ("EA", 3, 0, "S"), ("MA", 6, 0, ""), ("QA", 1, 2, ""), ("EA", 4, 0, "S"),
+    ("S1", 2, 2, ""), ("MA", 7, 0, ""), ("I", 1, 3, "V"), ("EA", 5, 0, "S"),
+    ("MA", 8, 0, ""), ("EA", 6, 0, "S"), ("S1", 4, 2, ""), ("MA", 9, 0, ""),
+    ("EA", 7, 0, "S"), ("QA", 1, 3, ""), ("MA", 10, 0, ""), ("EA", 8, 0, "S"),
+    ("S1", 6, 2, ""), ("Q", 7, 0, ""), ("MA", 11, 0, ""), ("EA", 9, 0, "S"),
+    ("I", 0, 3, "V"), ("M", 7, 0, ""), ("EA", 10, 0, "S"), ("S1", 8, 2, ""),
+    ("EA", 11, 0, "S"), ("QA", 0, 3, ""), ("E", 7, 0, "S"), ("S1", 10, 2, ""),
+    ("MA", 12, 0, ""), ("MA", 13, 0, ""), ("EA", 12, 0, "S"), ("S0", 3, 0, ""),
+    ("MA", 14, 0, ""), ("EA", 13, 0, "S"), ("MA", 15, 0, ""), ("EA", 14, 0, "S"),
+    ("S1", 12, 2, ""), ("EA", 15, 0, "S"), ("S1", 14, 1, ""), ("S1", 15, 1, ""),
+]
+
+def tile_middlelayer_v_kernel(tc, in_data, W, bias, z, grad_out, out_0, out_1):
+    nc = tc.nc
+    z_v = z.rearrange("(g p j) w -> p g j w", g=2, j=4)
+    g_v = grad_out.rearrange("(g p j) w o -> p g j (w o)", g=2, j=4)
+    x_v = in_data.rearrange("(g p j) c -> p g j c", g=2, j=4)
+    w_v = W.rearrange("(g p j) c -> p g j c", g=4, j=4)
+    o0_v = out_0.rearrange("(g p j) n -> p g j n", g=2, j=4)
+    o1_v = out_1.rearrange("(t m) k -> m t k", m=P)
+
+    with ExitStack() as ctx:
+        raw = ctx.enter_context(tc.tile_pool(name="raw", bufs=1))
+        keep = ctx.enter_context(tc.tile_pool(name="keep", bufs=1))
+        work = ctx.enter_context(tc.tile_pool(name="work", bufs=1))
+        psum = ctx.enter_context(tc.psum_pool(name="psum", bufs=8))
+        ctx.enter_context(tc.manual_schedule())
+
+        ident = keep.tile([P, P], F32, name="ident")
+        make_identity(nc, ident[:])
+        st0 = []
+        dz_n = []
+        for g in range(2):
+            t0 = keep.tile([P, 4, 512, 2], F32, name="st0_%d" % g)
+            nc.vector.memset(t0[:], 0.0)
+            st0.append(t0)
+            t1 = keep.tile([P, 4, 2048], BF16, name="dz_n%d" % g, align_bytes=64)
+            dz_n.append(t1)
+        w_codes = keep.tile([P, 4, 512], U32, name="w_codes", align_bytes=64)
+        w_scales = keep.tile([P, 4, 512], U8, name="w_scales", align_bytes=64)
+        x_codes = keep.tile([P, 2, 512], U32, name="x_codes", align_bytes=64)
+        x_scales = keep.tile([P, 2, 512], U8, name="x_scales", align_bytes=64)
+        a_codes = keep.tile([P, 2, 2048], U32, name="a_codes", align_bytes=64)
+        a_scales = keep.tile([P, 2, 2048], U8, name="a_scales", align_bytes=64)
+
+        tiles = {}
+
+        def copy_on(eng, out, in_):
+            if eng == "V":
+                nc.vector.tensor_copy(out=out, in_=in_)
+            else:
+                nc.scalar.copy(out=out, in_=in_)
+
+        def flat(grp):
+            return grp[:].rearrange("p c j -> p (c j)")
+
+        for kind, a, b, eng in ORDER:
+            if kind == "LW":
+                t = raw.tile([P, 4, 512], BF16, name="w_raw", tag="raw4", bufs=RAW4)
+                nc.sync.dma_start(out=t[:], in_=w_v[:, a, :, :])
+                tiles[("w", a)] = t
+            elif kind == "LG":
+                t = raw.tile([P, 2048], BF16, name="g_raw1", tag="raw4", bufs=RAW4)
+                nc.sync.dma_start(out=t[:], in_=g_v[:, 0, a, :])
+                tiles[("g", a)] = t[:]
+            elif kind == "Lg":
+                t = raw.tile([P, 2, 2048], BF16, name="g_raw2", tag="raw8", bufs=RAW8)
+                nc.sync.dma_start(out=t[:], in_=g_v[:, a // 2, 2 * (a % 2) : 2 * (a % 2) + 2, :])
+                tiles[("g", 2 * a)] = t[:, 0, :]
+                tiles[("g", 2 * a + 1)] = t[:, 1, :]
+            elif kind == "Lz":
+                t = raw.tile([P, 2048], F32, name="z_raw", tag="raw8", bufs=RAW8)
+                nc.sync.dma_start(out=t[:], in_=z_v[:, a // 4, a % 4, :])
+                tiles[("z", a)] = t
+            elif kind == "Lx":
+                t = raw.tile([P, 4, 1024], BF16, name="x_raw", tag="raw8", bufs=RAW8)
+                nc.sync.dma_start(out=t[:], in_=x_v[:, a, :, :])
+                tiles[("x", a)] = t
+            elif kind == "IW":
+                grp = work.tile([P, 512, 4], BF16, name="grp_w", tag="grp_w", bufs=2, align_bytes=64)
+                tiles[("gw", a)] = grp
+                src = tiles[("w", a)][:].rearrange("p j c -> p c j")
+                if a >= 2:
+                    nc.vector.tensor_scalar_mul(out=grp[:], in0=src, scalar1=-1.0)
+                else:
+                    copy_on(eng, grp[:], src)
+            elif kind == "QW":
+                nc.vector.quantize_mx(
+                    out=w_codes[:, a, :].bitcast(E4X4), scales=w_scales[:, a, :], in_=flat(tiles[("gw", a)])
+                )
+            elif kind == "IX":
+                grp = work.tile([P, 512, 4], BF16, name="grp_x", tag="grp_w", bufs=2, align_bytes=64)
+                tiles[("gx", a)] = grp
+                src = tiles[("x", a)][:].rearrange("p j (k e) -> p j k e", e=2)[:, :, :, 1].rearrange("p j k -> p k j")
+                copy_on(eng, grp[:], src)
+            elif kind == "QX":
+                nc.vector.quantize_mx(
+                    out=x_codes[:, a, :].bitcast(E4X4), scales=x_scales[:, a, :], in_=flat(tiles[("gx", a)])
+                )
+            elif kind == "D":
+                gr = tiles[("g", a)].rearrange("p (w e) -> p w e", e=2)[:, :, 0]
+                nc.vector.scalar_tensor_tensor(
+                    out=dz_n[a // 4][:, a % 4, :].rearrange("p (h w) -> p h w", h=2),
+                    in0=tiles[("z", a)][:].rearrange("p (h w) -> p h w", h=2),
+                    scalar=0.0,
+                    in1=gr.unsqueeze(1).to_broadcast([P, 2, 1024]),
+                    op0=ALU.is_gt,
+                    op1=ALU.mult,
+                )
+            elif kind == "T":
+                words = dz_n[a // 4][:, a % 4, :].bitcast(F32)
+                tp = psum.tile([P, 512], F32, name="tp", tag="bank")
+                tiles[("tp", a, b)] = tp
+                for gg in range(2):
+                    gp = 2 * b + gg
+                    for u in range(2):
+                        nc.tensor.transpose(
+                            tp[:, (2 * gg + u) * P : (2 * gg + u + 1) * P],
+                            words[:, 256 * gp + u : 256 * (gp + 1) : 2],
+                            ident[:],
+                        )
+            elif kind == "C":
+                if b == 0:
+                    grp = work.tile([P, 512, 4], BF16, name="grp_b", tag="grp_b", bufs=3, align_bytes=64)
+                    tiles[("gb", a)] = grp
+                grp_w = flat(tiles[("gb", a)]).bitcast(F32)
+                copy_on(
+                    eng,
+                    grp_w[:, 512 * b : 512 * (b + 1)].rearrange("p (s c u) -> p s c u", s=2, u=2),
+                    tiles[("tp", a, b)][:].rearrange("p (s u c) -> p s c u", s=2, u=2),
+                )
+            elif kind == "Q":
+                bc = work.tile([P, 512], U32, name="b_codes", tag="b_codes", bufs=3, align_bytes=64)
+                bs = work.tile([P, 512], U8, name="b_scales", tag="b_scales", bufs=3, align_bytes=64)
+                tiles[("bc", a)] = (bc, bs)
+                nc.vector.quantize_mx(out=bc[:].bitcast(E5X4), scales=bs[:], in_=flat(tiles[("gb", a)]))
+            elif kind == "M":
+                bc, bs = tiles[("bc", a)]
+                acc = psum.tile([P, 512], F32, name="acc0", tag="bank")
+                tiles[("acc0", a)] = acc
+                for gp in range(4):
+                    nc.tensor.matmul_mx(
+                        out=acc[:],
+                        lhsT=bc[:, P * gp : P * (gp + 1)].bitcast(E5X4),
+                        lhsT_scale=bs[:, P * gp : P * (gp + 1)],
+                        rhs=w_codes[:, gp, :].bitcast(E4X4),
+                        rhs_scale=w_scales[:, gp, :],
+                        start=(gp == 0),
+                        stop=(gp == 3),
+                    )
+            elif kind == "E":
+                copy_on(eng, st0[a // 4][:, a % 4, :, 1], tiles[("acc0", a)][:])
+            elif kind == "S0":
+                g = a // 2
+                j0 = 2 * (a % 2)
+                nc.sync.dma_start(
+                    out=o0_v[:, g, j0 : j0 + 2, :],
+                    in_=st0[g][:, j0 : j0 + 2, :, :].rearrange("p j k e -> p j (k e)"),
+                )
+            elif kind == "I":
+                grp = work.tile([P, 512, 4], BF16, name="grp_a", tag="grp_a", bufs=3, align_bytes=64)
+                tiles[("ga", a, b)] = grp
+                src = dz_n[a][:, :, 512 * b : 512 * (b + 1)].rearrange("p j w -> p w j")
+                if b >= 2:
+                    nc.vector.tensor_scalar_mul(out=grp[:], in0=src, scalar1=-1.0)
+                else:
+                    copy_on(eng, grp[:], src)
+            elif kind == "QA":
+                nc.vector.quantize_mx(
+                    out=a_codes[:, a, 512 * b : 512 * (b + 1)].bitcast(E5X4),
+                    scales=a_scales[:, a, 512 * b : 512 * (b + 1)],
+                    in_=flat(tiles[("ga", a, b)]),
+                )
+            elif kind == "MA":
+                acc = psum.tile([P, 512], F32, name="acc1", tag="bank")
+                tiles[("acc1", a)] = acc
+                for g in range(2):
+                    nc.tensor.matmul_mx(
+                        out=acc[:],
+                        lhsT=a_codes[:, g, P * a : P * (a + 1)].bitcast(E5X4),
+                        lhsT_scale=a_scales[:, g, P * a : P * (a + 1)],
+                        rhs=x_codes[:, g, :].bitcast(E4X4),
+                        rhs_scale=x_scales[:, g, :],
+                        start=(g == 0),
+                        stop=(g == 1),
+                    )
+            elif kind == "EA":
+                if ("st1", a // 4) not in tiles:
+                    st = raw.tile([P, 4, 512], F32, name="st1", tag="raw8", bufs=RAW8)
+                    tiles[("st1", a // 4)] = st
+                copy_on(eng, tiles[("st1", a // 4)][:, a % 4, :], tiles[("acc1", a)][:])
+            elif kind == "S1":
+                nc.sync.dma_start(
+                    out=o1_v[:, a : a + b, :], in_=tiles[("st1", a // 4)][:, a % 4 : a % 4 + b, :]
+                )

@@ -19,47 +19,48 @@ E5X4 = mybir.dt.float8_e5m2_x4
 ALU = mybir.AluOpType
 
 P = 128
-RAW8 = 9
+RAW8 = 11
 RAW4 = 6
 
 ORDER = [
-    ("LW", 0, 0, ""), ("LG", 0, 0, ""), ("Lz", 0, 0, ""), ("LW", 1, 0, ""),
-    ("LG", 1, 0, ""), ("Lz", 1, 0, ""), ("LW", 2, 0, ""), ("LW", 3, 0, ""),
-    ("Lg", 1, 0, ""), ("Lz", 2, 0, ""), ("Lz", 3, 0, ""), ("Lg", 2, 0, ""),
-    ("Lz", 4, 0, ""), ("Lz", 5, 0, ""), ("Lg", 3, 0, ""), ("IW", 0, 0, "S"),
-    ("QW", 0, 0, ""), ("D", 0, 0, ""), ("IW", 1, 0, "V"), ("Lz", 6, 0, ""),
-    ("T", 0, 0, ""), ("T", 0, 1, ""), ("C", 0, 0, "S"), ("QW", 1, 0, ""),
-    ("C", 0, 1, "S"), ("Q", 0, 0, ""), ("D", 1, 0, ""), ("IW", 2, 0, "V"),
-    ("Lz", 7, 0, ""), ("T", 1, 0, ""), ("T", 1, 1, ""), ("C", 1, 0, "S"),
-    ("QW", 2, 0, ""), ("C", 1, 1, "S"), ("IW", 3, 0, "V"), ("QW", 3, 0, ""),
-    ("Q", 1, 0, ""), ("M", 0, 0, ""), ("D", 2, 0, ""), ("M", 1, 0, ""),
-    ("E", 0, 0, "S"), ("D", 3, 0, ""), ("T", 2, 0, ""), ("E", 1, 0, "S"),
-    ("T", 2, 1, ""), ("C", 2, 0, "S"), ("S0", 0, 0, ""), ("I", 0, 2, "V"),
-    ("Lx", 0, 0, ""), ("T", 3, 0, ""), ("C", 2, 1, "S"), ("Lx", 1, 0, ""),
-    ("T", 3, 1, ""), ("I", 0, 0, "S"), ("Q", 2, 0, ""), ("D", 4, 0, ""),
-    ("M", 2, 0, ""), ("C", 3, 0, "S"), ("C", 3, 1, "S"), ("D", 5, 0, ""),
-    ("T", 4, 0, ""), ("E", 2, 0, "S"), ("T", 4, 1, ""), ("C", 4, 0, "S"),
-    ("Q", 3, 0, ""), ("C", 4, 1, "S"), ("T", 5, 0, ""), ("QA", 0, 0, ""),
-    ("T", 5, 1, ""), ("I", 0, 1, "S"), ("Q", 4, 0, ""), ("M", 3, 0, ""),
-    ("D", 6, 0, ""), ("M", 4, 0, ""), ("C", 5, 0, "S"), ("C", 5, 1, "S"),
-    ("D", 7, 0, ""), ("T", 6, 0, ""), ("E", 3, 0, "S"), ("T", 6, 1, ""),
-    ("C", 6, 0, "S"), ("S0", 1, 0, ""), ("Q", 5, 0, ""), ("T", 7, 0, ""),
-    ("C", 6, 1, "S"), ("QA", 0, 1, ""), ("T", 7, 1, ""), ("E", 4, 0, "S"),
-    ("Q", 6, 0, ""), ("M", 5, 0, ""), ("QA", 0, 2, ""), ("C", 7, 0, "S"),
-    ("IX", 0, 0, "V"), ("M", 6, 0, ""), ("I", 1, 0, "S"), ("QX", 0, 0, ""),
-    ("IX", 1, 0, "V"), ("C", 7, 1, "S"), ("QX", 1, 0, ""), ("E", 5, 0, "S"),
-    ("QA", 1, 0, ""), ("I", 1, 1, "V"), ("MA", 0, 0, ""), ("E", 6, 0, "S"),
-    ("MA", 1, 0, ""), ("S0", 2, 0, ""), ("MA", 2, 0, ""), ("EA", 0, 0, "V"),
-    ("MA", 3, 0, ""), ("QA", 1, 1, ""), ("EA", 1, 0, "S"), ("I", 1, 2, "V"),
-    ("MA", 4, 0, ""), ("EA", 2, 0, "S"), ("S1", 0, 2, ""), ("MA", 5, 0, ""),
-    ("EA", 3, 0, "S"), ("MA", 6, 0, ""), ("QA", 1, 2, ""), ("EA", 4, 0, "S"),
-    ("S1", 2, 2, ""), ("MA", 7, 0, ""), ("I", 1, 3, "V"), ("EA", 5, 0, "S"),
-    ("MA", 8, 0, ""), ("EA", 6, 0, "S"), ("S1", 4, 2, ""), ("MA", 9, 0, ""),
-    ("EA", 7, 0, "S"), ("QA", 1, 3, ""), ("MA", 10, 0, ""), ("EA", 8, 0, "S"),
-    ("S1", 6, 2, ""), ("Q", 7, 0, ""), ("MA", 11, 0, ""), ("EA", 9, 0, "S"),
-    ("I", 0, 3, "V"), ("M", 7, 0, ""), ("EA", 10, 0, "S"), ("S1", 8, 2, ""),
-    ("EA", 11, 0, "S"), ("QA", 0, 3, ""), ("E", 7, 0, "S"), ("S1", 10, 2, ""),
-    ("MA", 12, 0, ""), ("MA", 13, 0, ""), ("EA", 12, 0, "S"), ("S0", 3, 0, ""),
+    ("LW", 0, 0, ""), ("Z", 0, 0, "G"), ("LG", 0, 0, ""), ("Lz", 0, 0, ""),
+    ("LW", 1, 0, ""), ("LG", 1, 0, ""), ("Lz", 1, 0, ""), ("LW", 2, 0, ""),
+    ("LW", 3, 0, ""), ("Z", 1, 0, "G"), ("Z", 2, 0, "G"), ("Z", 3, 0, "G"),
+    ("Lg", 1, 0, ""), ("IW", 0, 0, "S"), ("Lz", 2, 0, ""), ("QW", 0, 0, ""),
+    ("Lz", 3, 0, ""), ("D", 0, 0, ""), ("Lg", 2, 0, ""), ("Lz", 4, 0, ""),
+    ("IW", 1, 0, "V"), ("T", 0, 0, ""), ("T", 0, 1, ""), ("C", 0, 0, "S"),
+    ("QW", 1, 0, ""), ("C", 0, 1, "S"), ("Lz", 5, 0, ""), ("D", 1, 0, ""),
+    ("Lg", 3, 0, ""), ("IW", 2, 0, "S"), ("Lz", 6, 0, ""), ("Q", 0, 0, ""),
+    ("T", 1, 0, ""), ("IW", 3, 0, "V"), ("T", 1, 1, ""), ("C", 1, 0, "S"),
+    ("C", 1, 1, "S"), ("QW", 2, 0, ""), ("Lz", 7, 0, ""), ("QW", 3, 0, ""),
+    ("Q", 1, 0, ""), ("M", 0, 0, ""), ("Lx", 0, 0, ""), ("D", 2, 0, ""),
+    ("M", 1, 0, ""), ("E", 0, 0, "S"), ("Lx", 1, 0, ""), ("D", 3, 0, ""),
+    ("T", 2, 0, ""), ("E", 1, 0, "S"), ("T", 2, 1, ""), ("C", 2, 0, "S"),
+    ("S0", 0, 0, ""), ("I", 0, 0, "V"), ("T", 3, 0, ""), ("C", 2, 1, "S"),
+    ("I", 0, 1, "S"), ("T", 3, 1, ""), ("Q", 2, 0, ""), ("QA", 0, 0, ""),
+    ("M", 2, 0, ""), ("D", 4, 0, ""), ("C", 3, 0, "S"), ("C", 3, 1, "S"),
+    ("E", 2, 0, "S"), ("Q", 3, 0, ""), ("T", 4, 0, ""), ("D", 5, 0, ""),
+    ("T", 4, 1, ""), ("C", 4, 0, "S"), ("M", 3, 0, ""), ("C", 4, 1, "S"),
+    ("Q", 4, 0, ""), ("QA", 0, 1, ""), ("T", 5, 0, ""), ("E", 3, 0, "S"),
+    ("I", 0, 2, "V"), ("T", 5, 1, ""), ("M", 4, 0, ""), ("C", 5, 0, "S"),
+    ("D", 6, 0, ""), ("S0", 1, 0, ""), ("C", 5, 1, "S"), ("Q", 5, 0, ""),
+    ("T", 6, 0, ""), ("D", 7, 0, ""), ("T", 6, 1, ""), ("C", 6, 0, "S"),
+    ("M", 5, 0, ""), ("C", 6, 1, "S"), ("Q", 6, 0, ""), ("I", 1, 0, "V"),
+    ("T", 7, 0, ""), ("T", 7, 1, ""), ("C", 7, 0, "S"), ("I", 1, 1, "V"),
+    ("M", 6, 0, ""), ("C", 7, 1, "S"), ("E", 4, 0, "S"), ("QA", 1, 0, ""),
+    ("QA", 1, 1, ""), ("Q", 7, 0, ""), ("E", 5, 0, "S"), ("IX", 0, 0, "V"),
+    ("M", 7, 0, ""), ("E", 6, 0, "S"), ("S0", 2, 0, ""), ("IX", 1, 0, "V"),
+    ("QX", 0, 0, ""), ("E", 7, 0, "S"), ("QX", 1, 0, ""), ("QA", 0, 2, ""),
+    ("MA", 0, 0, ""), ("S0", 3, 0, ""), ("I", 1, 2, "V"), ("MA", 1, 0, ""),
+    ("EA", 0, 0, "S"), ("MA", 2, 0, ""), ("EA", 1, 0, "S"), ("I", 1, 3, "V"),
+    ("MA", 3, 0, ""), ("EA", 2, 0, "S"), ("S1", 0, 2, ""), ("MA", 4, 0, ""),
+    ("EA", 3, 0, "S"), ("QA", 1, 2, ""), ("MA", 5, 0, ""), ("EA", 4, 0, "S"),
+    ("S1", 2, 2, ""), ("QA", 1, 3, ""), ("MA", 6, 0, ""), ("EA", 5, 0, "S"),
+    ("I", 0, 3, "V"), ("MA", 7, 0, ""), ("EA", 6, 0, "S"), ("S1", 4, 2, ""),
+    ("MA", 8, 0, ""), ("EA", 7, 0, "S"), ("QA", 0, 3, ""), ("MA", 9, 0, ""),
+    ("EA", 8, 0, "S"), ("S1", 6, 2, ""), ("MA", 10, 0, ""), ("EA", 9, 0, "S"),
+    ("MA", 11, 0, ""), ("EA", 10, 0, "S"), ("S1", 8, 2, ""), ("MA", 12, 0, ""),
+    ("EA", 11, 0, "S"), ("MA", 13, 0, ""), ("EA", 12, 0, "S"), ("S1", 10, 2, ""),
     ("MA", 14, 0, ""), ("EA", 13, 0, "S"), ("MA", 15, 0, ""), ("EA", 14, 0, "S"),
     ("S1", 12, 2, ""), ("EA", 15, 0, "S"), ("S1", 14, 1, ""), ("S1", 15, 1, ""),
 ]
@@ -85,8 +86,7 @@ def tile_middlelayer_v_kernel(tc, in_data, W, bias, z, grad_out, out_0, out_1):
         st0 = []
         dz_n = []
         for g in range(2):
-            t0 = keep.tile([P, 4, 512, 2], F32, name="st0_%d" % g)
-            nc.vector.memset(t0[:], 0.0)
+            t0 = keep.tile([P, 2, 512, 2], F32, name="st0_%d" % g)
             st0.append(t0)
             t1 = keep.tile([P, 4, 2048], BF16, name="dz_n%d" % g, align_bytes=64)
             dz_n.append(t1)
@@ -109,7 +109,9 @@ def tile_middlelayer_v_kernel(tc, in_data, W, bias, z, grad_out, out_0, out_1):
             return grp[:].rearrange("p c j -> p (c j)")
 
         for kind, a, b, eng in ORDER:
-            if kind == "LW":
+            if kind == "Z":
+                nc.gpsimd.memset(st0[a // 2][:, a % 2, :, :], 0.0)
+            elif kind == "LW":
                 t = raw.tile([P, 4, 512], BF16, name="w_raw", tag="raw4", bufs=RAW4)
                 nc.sync.dma_start(out=t[:], in_=w_v[:, a, :, :])
                 tiles[("w", a)] = t
@@ -134,8 +136,10 @@ def tile_middlelayer_v_kernel(tc, in_data, W, bias, z, grad_out, out_0, out_1):
                 grp = work.tile([P, 512, 4], BF16, name="grp_w", tag="grp_w", bufs=2, align_bytes=64)
                 tiles[("gw", a)] = grp
                 src = tiles[("w", a)][:].rearrange("p j c -> p c j")
-                if a >= 2:
+                if a >= 2 and eng == "V":
                     nc.vector.tensor_scalar_mul(out=grp[:], in0=src, scalar1=-1.0)
+                elif a >= 2:
+                    nc.scalar.mul(out=grp[:], in_=src, mul=-1.0)
                 else:
                     copy_on(eng, grp[:], src)
             elif kind == "QW":
@@ -203,13 +207,13 @@ def tile_middlelayer_v_kernel(tc, in_data, W, bias, z, grad_out, out_0, out_1):
                         stop=(gp == 3),
                     )
             elif kind == "E":
-                copy_on(eng, st0[a // 4][:, a % 4, :, 1], tiles[("acc0", a)][:])
+                copy_on(eng, st0[(a // 2) % 2][:, a % 2, :, 1], tiles[("acc0", a)][:])
             elif kind == "S0":
                 g = a // 2
                 j0 = 2 * (a % 2)
                 nc.sync.dma_start(
                     out=o0_v[:, g, j0 : j0 + 2, :],
-                    in_=st0[g][:, j0 : j0 + 2, :, :].rearrange("p j k e -> p j (k e)"),
+                    in_=st0[a % 2][:].rearrange("p j k e -> p j (k e)"),
                 )
             elif kind == "I":
                 grp = work.tile([P, 512, 4], BF16, name="grp_a", tag="grp_a", bufs=3, align_bytes=64)

@@ -19,48 +19,49 @@ E5X4 = mybir.dt.float8_e5m2_x4
 ALU = mybir.AluOpType
 
 P = 128
-RAW8 = 11
+RAW8 = 9
 RAW4 = 6
 
 ORDER = [
-    ("LW", 0, 0, ""), ("Z", 0, 0, "G"), ("LG", 0, 0, ""), ("Lz", 0, 0, ""),
-    ("LW", 1, 0, ""), ("LG", 1, 0, ""), ("Lz", 1, 0, ""), ("LW", 2, 0, ""),
-    ("LW", 3, 0, ""), ("Z", 1, 0, "G"), ("Z", 2, 0, "G"), ("Z", 3, 0, "G"),
+    ("LW", 0, 0, ""), ("Z", 0, 0, "S"), ("Z", 4, 0, "G"), ("LG", 0, 0, ""),
+    ("Lz", 0, 0, ""), ("LW", 1, 0, ""), ("LG", 1, 0, ""), ("Lz", 1, 0, ""),
+    ("LW", 2, 0, ""), ("LW", 3, 0, ""), ("Z", 1, 0, "S"), ("Z", 5, 0, "G"),
+    ("Z", 2, 0, "S"), ("Z", 6, 0, "G"), ("Z", 3, 0, "S"), ("Z", 7, 0, "G"),
     ("Lg", 1, 0, ""), ("IW", 0, 0, "S"), ("Lz", 2, 0, ""), ("QW", 0, 0, ""),
     ("Lz", 3, 0, ""), ("D", 0, 0, ""), ("Lg", 2, 0, ""), ("Lz", 4, 0, ""),
     ("IW", 1, 0, "V"), ("T", 0, 0, ""), ("T", 0, 1, ""), ("C", 0, 0, "S"),
-    ("QW", 1, 0, ""), ("C", 0, 1, "S"), ("Lz", 5, 0, ""), ("D", 1, 0, ""),
-    ("Lg", 3, 0, ""), ("IW", 2, 0, "S"), ("Lz", 6, 0, ""), ("Q", 0, 0, ""),
-    ("T", 1, 0, ""), ("IW", 3, 0, "V"), ("T", 1, 1, ""), ("C", 1, 0, "S"),
-    ("C", 1, 1, "S"), ("QW", 2, 0, ""), ("Lz", 7, 0, ""), ("QW", 3, 0, ""),
-    ("Q", 1, 0, ""), ("M", 0, 0, ""), ("Lx", 0, 0, ""), ("D", 2, 0, ""),
-    ("M", 1, 0, ""), ("E", 0, 0, "S"), ("Lx", 1, 0, ""), ("D", 3, 0, ""),
-    ("T", 2, 0, ""), ("E", 1, 0, "S"), ("T", 2, 1, ""), ("C", 2, 0, "S"),
-    ("S0", 0, 0, ""), ("I", 0, 0, "V"), ("T", 3, 0, ""), ("C", 2, 1, "S"),
-    ("I", 0, 1, "S"), ("T", 3, 1, ""), ("Q", 2, 0, ""), ("QA", 0, 0, ""),
-    ("M", 2, 0, ""), ("D", 4, 0, ""), ("C", 3, 0, "S"), ("C", 3, 1, "S"),
+    ("QW", 1, 0, ""), ("C", 0, 1, "S"), ("Lz", 5, 0, ""), ("Q", 0, 0, ""),
+    ("D", 1, 0, ""), ("Lg", 3, 0, ""), ("IW", 2, 0, "S"), ("Lz", 6, 0, ""),
+    ("IW", 3, 0, "V"), ("T", 1, 0, ""), ("T", 1, 1, ""), ("C", 1, 0, "S"),
+    ("QW", 2, 0, ""), ("C", 1, 1, "S"), ("Lz", 7, 0, ""), ("QW", 3, 0, ""),
+    ("Q", 1, 0, ""), ("M", 0, 0, ""), ("D", 2, 0, ""), ("M", 1, 0, ""),
+    ("E", 0, 0, "S"), ("E", 1, 0, "S"), ("T", 2, 0, ""), ("D", 3, 0, ""),
+    ("T", 2, 1, ""), ("C", 2, 0, "S"), ("S0", 0, 0, ""), ("C", 2, 1, "S"),
+    ("I", 0, 0, "V"), ("Lx", 0, 0, ""), ("T", 3, 0, ""), ("I", 0, 1, "S"),
+    ("Lx", 1, 0, ""), ("T", 3, 1, ""), ("Q", 2, 0, ""), ("QA", 0, 0, ""),
+    ("M", 2, 0, ""), ("C", 3, 0, "S"), ("D", 4, 0, ""), ("C", 3, 1, "S"),
     ("E", 2, 0, "S"), ("Q", 3, 0, ""), ("T", 4, 0, ""), ("D", 5, 0, ""),
     ("T", 4, 1, ""), ("C", 4, 0, "S"), ("M", 3, 0, ""), ("C", 4, 1, "S"),
     ("Q", 4, 0, ""), ("QA", 0, 1, ""), ("T", 5, 0, ""), ("E", 3, 0, "S"),
-    ("I", 0, 2, "V"), ("T", 5, 1, ""), ("M", 4, 0, ""), ("C", 5, 0, "S"),
-    ("D", 6, 0, ""), ("S0", 1, 0, ""), ("C", 5, 1, "S"), ("Q", 5, 0, ""),
-    ("T", 6, 0, ""), ("D", 7, 0, ""), ("T", 6, 1, ""), ("C", 6, 0, "S"),
-    ("M", 5, 0, ""), ("C", 6, 1, "S"), ("Q", 6, 0, ""), ("I", 1, 0, "V"),
-    ("T", 7, 0, ""), ("T", 7, 1, ""), ("C", 7, 0, "S"), ("I", 1, 1, "V"),
-    ("M", 6, 0, ""), ("C", 7, 1, "S"), ("E", 4, 0, "S"), ("QA", 1, 0, ""),
-    ("QA", 1, 1, ""), ("Q", 7, 0, ""), ("E", 5, 0, "S"), ("IX", 0, 0, "V"),
-    ("M", 7, 0, ""), ("E", 6, 0, "S"), ("S0", 2, 0, ""), ("IX", 1, 0, "V"),
-    ("QX", 0, 0, ""), ("E", 7, 0, "S"), ("QX", 1, 0, ""), ("QA", 0, 2, ""),
-    ("MA", 0, 0, ""), ("S0", 3, 0, ""), ("I", 1, 2, "V"), ("MA", 1, 0, ""),
-    ("EA", 0, 0, "S"), ("MA", 2, 0, ""), ("EA", 1, 0, "S"), ("I", 1, 3, "V"),
-    ("MA", 3, 0, ""), ("EA", 2, 0, "S"), ("S1", 0, 2, ""), ("MA", 4, 0, ""),
-    ("EA", 3, 0, "S"), ("QA", 1, 2, ""), ("MA", 5, 0, ""), ("EA", 4, 0, "S"),
-    ("S1", 2, 2, ""), ("QA", 1, 3, ""), ("MA", 6, 0, ""), ("EA", 5, 0, "S"),
-    ("I", 0, 3, "V"), ("MA", 7, 0, ""), ("EA", 6, 0, "S"), ("S1", 4, 2, ""),
-    ("MA", 8, 0, ""), ("EA", 7, 0, "S"), ("QA", 0, 3, ""), ("MA", 9, 0, ""),
-    ("EA", 8, 0, "S"), ("S1", 6, 2, ""), ("MA", 10, 0, ""), ("EA", 9, 0, "S"),
-    ("MA", 11, 0, ""), ("EA", 10, 0, "S"), ("S1", 8, 2, ""), ("MA", 12, 0, ""),
-    ("EA", 11, 0, "S"), ("MA", 13, 0, ""), ("EA", 12, 0, "S"), ("S1", 10, 2, ""),
+    ("I", 0, 2, "V"), ("M", 4, 0, ""), ("C", 5, 0, "S"), ("D", 6, 0, ""),
+    ("S0", 1, 0, ""), ("T", 5, 1, ""), ("E", 4, 0, "S"), ("D", 7, 0, ""),
+    ("T", 6, 0, ""), ("C", 5, 1, "S"), ("T", 6, 1, ""), ("C", 6, 0, "S"),
+    ("C", 6, 1, "S"), ("Q", 5, 0, ""), ("T", 7, 0, ""), ("Q", 6, 0, ""),
+    ("T", 7, 1, ""), ("C", 7, 0, "S"), ("I", 1, 0, "V"), ("M", 5, 0, ""),
+    ("C", 7, 1, "S"), ("IX", 0, 0, "V"), ("M", 6, 0, ""), ("E", 5, 0, "S"),
+    ("Q", 7, 0, ""), ("QX", 0, 0, ""), ("M", 7, 0, ""), ("IX", 1, 0, "V"),
+    ("E", 6, 0, "S"), ("S0", 2, 0, ""), ("QA", 1, 0, ""), ("E", 7, 0, "S"),
+    ("QX", 1, 0, ""), ("I", 1, 1, "V"), ("MA", 0, 0, ""), ("S0", 3, 0, ""),
+    ("MA", 1, 0, ""), ("EA", 0, 0, "S"), ("QA", 0, 2, ""), ("MA", 2, 0, ""),
+    ("EA", 1, 0, "S"), ("QA", 1, 1, ""), ("MA", 3, 0, ""), ("EA", 2, 0, "S"),
+    ("I", 1, 2, "V"), ("S1", 0, 2, ""), ("MA", 4, 0, ""), ("EA", 3, 0, "S"),
+    ("MA", 5, 0, ""), ("EA", 4, 0, "S"), ("S1", 2, 2, ""), ("I", 1, 3, "V"),
+    ("MA", 6, 0, ""), ("EA", 5, 0, "S"), ("MA", 7, 0, ""), ("EA", 6, 0, "S"),
+    ("S1", 4, 2, ""), ("QA", 1, 2, ""), ("EA", 7, 0, "S"), ("QA", 1, 3, ""),
+    ("MA", 8, 0, ""), ("S1", 6, 2, ""), ("I", 0, 3, "V"), ("MA", 9, 0, ""),
+    ("EA", 8, 0, "S"), ("MA", 10, 0, ""), ("EA", 9, 0, "S"), ("QA", 0, 3, ""),
+    ("MA", 11, 0, ""), ("EA", 10, 0, "S"), ("S1", 8, 2, ""), ("EA", 11, 0, "S"),
+    ("MA", 12, 0, ""), ("MA", 13, 0, ""), ("S1", 10, 2, ""), ("EA", 12, 0, "S"),
     ("MA", 14, 0, ""), ("EA", 13, 0, "S"), ("MA", 15, 0, ""), ("EA", 14, 0, "S"),
     ("S1", 12, 2, ""), ("EA", 15, 0, "S"), ("S1", 14, 1, ""), ("S1", 15, 1, ""),
 ]
@@ -83,11 +84,14 @@ def tile_middlelayer_v_kernel(tc, in_data, W, bias, z, grad_out, out_0, out_1):
 
         ident = keep.tile([P, P], F32, name="ident")
         make_identity(nc, ident[:])
+        zero = keep.tile([P, 1], F32, name="zero")
+        nc.gpsimd.memset(zero[:], 0.0)
         st0 = []
+        for k in range(4):
+            t0 = keep.tile([P, 2, 512, 2], F32, name="st0_%d" % k)
+            st0.append(t0)
         dz_n = []
         for g in range(2):
-            t0 = keep.tile([P, 2, 512, 2], F32, name="st0_%d" % g)
-            st0.append(t0)
             t1 = keep.tile([P, 4, 2048], BF16, name="dz_n%d" % g, align_bytes=64)
             dz_n.append(t1)
         w_codes = keep.tile([P, 4, 512], U32, name="w_codes", align_bytes=64)
@@ -110,7 +114,13 @@ def tile_middlelayer_v_kernel(tc, in_data, W, bias, z, grad_out, out_0, out_1):
 
         for kind, a, b, eng in ORDER:
             if kind == "Z":
-                nc.gpsimd.memset(st0[a // 2][:, a % 2, :, :], 0.0)
+                if eng == "S":
+                    nc.scalar.copy(
+                        out=st0[a // 2][:, a % 2, :, :].rearrange("p k e -> p (k e)"),
+                        in_=zero[:, 0:1].to_broadcast([P, 1024]),
+                    )
+                else:
+                    nc.gpsimd.memset(st0[a // 2][:, a % 2, :, :], 0.0)
             elif kind == "LW":
                 t = raw.tile([P, 4, 512], BF16, name="w_raw", tag="raw4", bufs=RAW4)
                 nc.sync.dma_start(out=t[:], in_=w_v[:, a, :, :])
@@ -207,13 +217,13 @@ def tile_middlelayer_v_kernel(tc, in_data, W, bias, z, grad_out, out_0, out_1):
                         stop=(gp == 3),
                     )
             elif kind == "E":
-                copy_on(eng, st0[(a // 2) % 2][:, a % 2, :, 1], tiles[("acc0", a)][:])
+                copy_on(eng, st0[a // 2][:, a % 2, :, 1], tiles[("acc0", a)][:])
             elif kind == "S0":
                 g = a // 2
                 j0 = 2 * (a % 2)
                 nc.sync.dma_start(
                     out=o0_v[:, g, j0 : j0 + 2, :],
-                    in_=st0[a % 2][:].rearrange("p j k e -> p j (k e)"),
+                    in_=st0[a][:].rearrange("p j k e -> p j (k e)"),
                 )
             elif kind == "I":
                 grp = work.tile([P, 512, 4], BF16, name="grp_a", tag="grp_a", bufs=3, align_bytes=64)

@@ -3,261 +3,318 @@ from contextlib import ExitStack
 import concourse.mybir as mybir
 from concourse.masks import make_identity
 
-B, EN_MID, DE_MID = 1024, 1024, 2048
-K1 = EN_MID // 2
-K2 = DE_MID // 2
+TOKENS, FEATURES, K_IN = 1024, 2048, 512
+HALF = FEATURES // 2
 
-FLOPS = 2 * 2 * B * DE_MID * K1
-BYTES = B * K1 * 2 + DE_MID * K1 * 2 + B * DE_MID * 4 + B * K2 * 2 + B * EN_MID * 4 + DE_MID * K1 * 4
+FLOPS = 2 * 2 * TOKENS * FEATURES * K_IN
+BYTES = 2 * TOKENS * K_IN + 2 * FEATURES * K_IN + 4 * TOKENS * FEATURES + 2 * TOKENS * HALF + 4 * TOKENS * 2 * K_IN + 4 * FEATURES * K_IN
 
 F32 = mybir.dt.float32
 BF16 = mybir.dt.bfloat16
 U32 = mybir.dt.uint32
 U8 = mybir.dt.uint8
-E4X4 = mybir.dt.float8_e4m3fn_x4
-E5X4 = mybir.dt.float8_e5m2_x4
+E4M3_X4 = mybir.dt.float8_e4m3fn_x4
+E5M2_X4 = mybir.dt.float8_e5m2_x4
 ALU = mybir.AluOpType
 
 P = 128
-RAW8 = 9
-RAW4 = 6
+PACK = 4
+PASS = P * PACK
+BANK = 512
 
-ORDER = [
-    ("LW", 0, 0, ""), ("Z", 0, 0, "S"), ("Z", 4, 0, "G"), ("LG", 0, 0, ""),
-    ("Lz", 0, 0, ""), ("LW", 1, 0, ""), ("LG", 1, 0, ""), ("Lz", 1, 0, ""),
-    ("LW", 2, 0, ""), ("LW", 3, 0, ""), ("Z", 1, 0, "S"), ("Z", 5, 0, "G"),
-    ("Z", 2, 0, "S"), ("Z", 6, 0, "G"), ("Z", 3, 0, "S"), ("Z", 7, 0, "G"),
-    ("Lg", 1, 0, ""), ("IW", 0, 0, "S"), ("Lz", 2, 0, ""), ("QW", 0, 0, ""),
-    ("Lz", 3, 0, ""), ("D", 0, 0, ""), ("Lg", 2, 0, ""), ("Lz", 4, 0, ""),
-    ("IW", 1, 0, "V"), ("T", 0, 0, ""), ("T", 0, 1, ""), ("C", 0, 0, "S"),
-    ("QW", 1, 0, ""), ("C", 0, 1, "S"), ("Lz", 5, 0, ""), ("Q", 0, 0, ""),
-    ("D", 1, 0, ""), ("Lg", 3, 0, ""), ("IW", 2, 0, "S"), ("Lz", 6, 0, ""),
-    ("IW", 3, 0, "V"), ("T", 1, 0, ""), ("T", 1, 1, ""), ("C", 1, 0, "S"),
-    ("QW", 2, 0, ""), ("C", 1, 1, "S"), ("Lz", 7, 0, ""), ("QW", 3, 0, ""),
-    ("Q", 1, 0, ""), ("M", 0, 0, ""), ("D", 2, 0, ""), ("M", 1, 0, ""),
-    ("E", 0, 0, "S"), ("E", 1, 0, "S"), ("T", 2, 0, ""), ("D", 3, 0, ""),
-    ("T", 2, 1, ""), ("C", 2, 0, "S"), ("S0", 0, 0, ""), ("C", 2, 1, "S"),
-    ("I", 0, 0, "V"), ("Lx", 0, 0, ""), ("T", 3, 0, ""), ("I", 0, 1, "S"),
-    ("Lx", 1, 0, ""), ("T", 3, 1, ""), ("Q", 2, 0, ""), ("QA", 0, 0, ""),
-    ("M", 2, 0, ""), ("C", 3, 0, "S"), ("D", 4, 0, ""), ("C", 3, 1, "S"),
-    ("E", 2, 0, "S"), ("Q", 3, 0, ""), ("T", 4, 0, ""), ("D", 5, 0, ""),
-    ("T", 4, 1, ""), ("C", 4, 0, "S"), ("M", 3, 0, ""), ("C", 4, 1, "S"),
-    ("Q", 4, 0, ""), ("QA", 0, 1, ""), ("T", 5, 0, ""), ("E", 3, 0, "S"),
-    ("I", 0, 2, "V"), ("M", 4, 0, ""), ("C", 5, 0, "S"), ("D", 6, 0, ""),
-    ("S0", 1, 0, ""), ("T", 5, 1, ""), ("E", 4, 0, "S"), ("D", 7, 0, ""),
-    ("T", 6, 0, ""), ("C", 5, 1, "S"), ("T", 6, 1, ""), ("C", 6, 0, "S"),
-    ("C", 6, 1, "S"), ("Q", 5, 0, ""), ("T", 7, 0, ""), ("Q", 6, 0, ""),
-    ("T", 7, 1, ""), ("C", 7, 0, "S"), ("I", 1, 0, "V"), ("M", 5, 0, ""),
-    ("C", 7, 1, "S"), ("IX", 0, 0, "V"), ("M", 6, 0, ""), ("E", 5, 0, "S"),
-    ("Q", 7, 0, ""), ("QX", 0, 0, ""), ("M", 7, 0, ""), ("IX", 1, 0, "V"),
-    ("E", 6, 0, "S"), ("S0", 2, 0, ""), ("QA", 1, 0, ""), ("E", 7, 0, "S"),
-    ("QX", 1, 0, ""), ("I", 1, 1, "V"), ("MA", 0, 0, ""), ("S0", 3, 0, ""),
-    ("MA", 1, 0, ""), ("EA", 0, 0, "S"), ("QA", 0, 2, ""), ("MA", 2, 0, ""),
-    ("EA", 1, 0, "S"), ("QA", 1, 1, ""), ("MA", 3, 0, ""), ("EA", 2, 0, "S"),
-    ("I", 1, 2, "V"), ("S1", 0, 2, ""), ("MA", 4, 0, ""), ("EA", 3, 0, "S"),
-    ("MA", 5, 0, ""), ("EA", 4, 0, "S"), ("S1", 2, 2, ""), ("I", 1, 3, "V"),
-    ("MA", 6, 0, ""), ("EA", 5, 0, "S"), ("MA", 7, 0, ""), ("EA", 6, 0, "S"),
-    ("S1", 4, 2, ""), ("QA", 1, 2, ""), ("EA", 7, 0, "S"), ("QA", 1, 3, ""),
-    ("MA", 8, 0, ""), ("S1", 6, 2, ""), ("I", 0, 3, "V"), ("MA", 9, 0, ""),
-    ("EA", 8, 0, "S"), ("MA", 10, 0, ""), ("EA", 9, 0, "S"), ("QA", 0, 3, ""),
-    ("MA", 11, 0, ""), ("EA", 10, 0, "S"), ("S1", 8, 2, ""), ("EA", 11, 0, "S"),
-    ("MA", 12, 0, ""), ("MA", 13, 0, ""), ("S1", 10, 2, ""), ("EA", 12, 0, "S"),
-    ("MA", 14, 0, ""), ("EA", 13, 0, "S"), ("MA", 15, 0, ""), ("EA", 14, 0, "S"),
-    ("S1", 12, 2, ""), ("EA", 15, 0, "S"), ("S1", 14, 1, ""), ("S1", 15, 1, ""),
-]
+BIG_SLOTS = 11
+SMALL_SLOTS = 6
+
 
 def tile_middlelayer_v_kernel(tc, in_data, W, bias, z, grad_out, out_0, out_1):
     nc = tc.nc
-    z_v = z.rearrange("(g p j) w -> p g j w", g=2, j=4)
-    g_v = grad_out.rearrange("(g p j) w o -> p g j (w o)", g=2, j=4)
-    x_v = in_data.rearrange("(g p j) c -> p g j c", g=2, j=4)
-    w_v = W.rearrange("(g p j) c -> p g j c", g=4, j=4)
-    o0_v = out_0.rearrange("(g p j) n -> p g j n", g=2, j=4)
-    o1_v = out_1.rearrange("(t m) k -> m t k", m=P)
+    z_view = z.rearrange("(g p j) f -> p g j f", g=2, j=PACK)
+    go_view = grad_out.rearrange("(g p j) f o -> p g j (f o)", g=2, j=PACK)
+    in_view = in_data.rearrange("(g p j) c -> p g j c", g=2, j=PACK)
+    w_view = W.rearrange("(f p j) k -> p f j k", f=4, j=PACK)
+    out_0_view = out_0.rearrange("(g p j) c -> p g j c", g=2, j=PACK)
+    out_1_view = out_1.rearrange("(t m) k -> m t k", m=P)
 
     with ExitStack() as ctx:
-        raw = ctx.enter_context(tc.tile_pool(name="raw", bufs=1))
+        loads = ctx.enter_context(tc.tile_pool(name="loads", bufs=1))
         keep = ctx.enter_context(tc.tile_pool(name="keep", bufs=1))
         work = ctx.enter_context(tc.tile_pool(name="work", bufs=1))
         psum = ctx.enter_context(tc.psum_pool(name="psum", bufs=8))
         ctx.enter_context(tc.manual_schedule())
 
-        ident = keep.tile([P, P], F32, name="ident")
-        make_identity(nc, ident[:])
-        zero = keep.tile([P, 1], F32, name="zero")
-        nc.gpsimd.memset(zero[:], 0.0)
-        st0 = []
-        for k in range(4):
-            t0 = keep.tile([P, 2, 512, 2], F32, name="st0_%d" % k)
-            st0.append(t0)
-        dz_n = []
+        identity = keep.tile([P, P], F32, name="identity")
+        make_identity(nc, identity[:])
+
+        s_tok = []
         for g in range(2):
-            t1 = keep.tile([P, 4, 2048], BF16, name="dz_n%d" % g, align_bytes=64)
-            dz_n.append(t1)
-        w_codes = keep.tile([P, 4, 512], U32, name="w_codes", align_bytes=64)
-        w_scales = keep.tile([P, 4, 512], U8, name="w_scales", align_bytes=64)
-        x_codes = keep.tile([P, 2, 512], U32, name="x_codes", align_bytes=64)
-        x_scales = keep.tile([P, 2, 512], U8, name="x_scales", align_bytes=64)
-        a_codes = keep.tile([P, 2, 2048], U32, name="a_codes", align_bytes=64)
-        a_scales = keep.tile([P, 2, 2048], U8, name="a_scales", align_bytes=64)
+            s_half = keep.tile([P, PACK, FEATURES], BF16, name="s_tok%d" % g, align_bytes=64)
+            s_tok.append(s_half)
+        dx_stage = []
+        for i in range(2):
+            stage = keep.tile([P, 2, K_IN, 2], F32, name="dx_stage%d" % i)
+            dx_stage.append(stage)
+        w_codes = keep.tile([P, 4, K_IN], U32, name="w_codes", align_bytes=64)
+        w_scales = keep.tile([P, 4, K_IN], U8, name="w_scales", align_bytes=64)
+        x_codes = keep.tile([P, 2, K_IN], U32, name="x_codes", align_bytes=64)
+        x_scales = keep.tile([P, 2, K_IN], U8, name="x_scales", align_bytes=64)
+        dz_codes = keep.tile([P, 2, FEATURES], U32, name="dz_codes", align_bytes=64)
+        dz_scales = keep.tile([P, 2, FEATURES], U8, name="dz_scales", align_bytes=64)
 
-        tiles = {}
+        w_raw, go_raw, z_raw, in_raw = {}, {}, {}, {}
+        w_grouped, x_grouped, dz_grouped, dzT_grouped = {}, {}, {}, {}
+        dzT_banks, dzT_codes, dx_bank, dw_bank, dw_stage = {}, {}, {}, {}, {}
 
-        def copy_on(eng, out, in_):
-            if eng == "V":
-                nc.vector.tensor_copy(out=out, in_=in_)
+        def load_w(f):
+            w_raw[f] = loads.tile([P, PACK, K_IN], BF16, name="w_raw", tag="small", bufs=SMALL_SLOTS)
+            nc.sync.dma_start(out=w_raw[f][:], in_=w_view[:, f, :, :])
+
+        def load_go_tile(c):
+            tile_c = loads.tile([P, FEATURES], BF16, name="go_raw1", tag="small", bufs=SMALL_SLOTS)
+            nc.sync.dma_start(out=tile_c[:], in_=go_view[:, c // PACK, c % PACK, :])
+            go_raw[c] = tile_c[:]
+
+        def load_go_pair(c):
+            pair = loads.tile([P, 2, FEATURES], BF16, name="go_raw2", tag="big", bufs=BIG_SLOTS)
+            nc.sync.dma_start(out=pair[:], in_=go_view[:, c // PACK, c % PACK : c % PACK + 2, :])
+            go_raw[c] = pair[:, 0, :]
+            go_raw[c + 1] = pair[:, 1, :]
+
+        def load_z(c):
+            z_raw[c] = loads.tile([P, FEATURES], F32, name="z_raw", tag="big", bufs=BIG_SLOTS)
+            nc.sync.dma_start(out=z_raw[c][:], in_=z_view[:, c // PACK, c % PACK, :])
+
+        def load_in(g):
+            in_raw[g] = loads.tile([P, PACK, 2 * K_IN], BF16, name="in_raw", tag="big", bufs=BIG_SLOTS)
+            nc.sync.dma_start(out=in_raw[g][:], in_=in_view[:, g, :, :])
+
+        def group(engine, tag, bufs, rows, negate):
+            grouped = work.tile([P, BANK, PACK], BF16, name=tag, tag=tag, bufs=bufs, align_bytes=64)
+            src = rows.rearrange("p j (c i) -> p c j i", i=4)
+            dst = grouped[:].rearrange("p (c i) j -> p c j i", i=4)
+            if engine == "vector" and negate:
+                nc.vector.tensor_scalar_mul(out=dst, in0=src, scalar1=-1.0)
+            elif engine == "vector":
+                nc.vector.tensor_copy(out=dst, in_=src)
+            elif negate:
+                nc.scalar.mul(out=dst, in_=src, mul=-1.0)
             else:
-                nc.scalar.copy(out=out, in_=in_)
+                nc.scalar.copy(out=dst, in_=src)
+            return grouped
 
-        def flat(grp):
-            return grp[:].rearrange("p c j -> p (c j)")
+        def quantize(grouped, codes, scales, fmt):
+            nc.vector.quantize_mx(
+                out=codes.bitcast(fmt), scales=scales, in_=grouped[:].rearrange("p c j -> p (c j)")
+            )
 
-        for kind, a, b, eng in ORDER:
-            if kind == "Z":
-                if eng == "S":
-                    nc.scalar.copy(
-                        out=st0[a // 2][:, a % 2, :, :].rearrange("p k e -> p (k e)"),
-                        in_=zero[:, 0:1].to_broadcast([P, 1024]),
-                    )
-                else:
-                    nc.gpsimd.memset(st0[a // 2][:, a % 2, :, :], 0.0)
-            elif kind == "LW":
-                t = raw.tile([P, 4, 512], BF16, name="w_raw", tag="raw4", bufs=RAW4)
-                nc.sync.dma_start(out=t[:], in_=w_v[:, a, :, :])
-                tiles[("w", a)] = t
-            elif kind == "LG":
-                t = raw.tile([P, 2048], BF16, name="g_raw1", tag="raw4", bufs=RAW4)
-                nc.sync.dma_start(out=t[:], in_=g_v[:, 0, a, :])
-                tiles[("g", a)] = t[:]
-            elif kind == "Lg":
-                t = raw.tile([P, 2, 2048], BF16, name="g_raw2", tag="raw8", bufs=RAW8)
-                nc.sync.dma_start(out=t[:], in_=g_v[:, a // 2, 2 * (a % 2) : 2 * (a % 2) + 2, :])
-                tiles[("g", 2 * a)] = t[:, 0, :]
-                tiles[("g", 2 * a + 1)] = t[:, 1, :]
-            elif kind == "Lz":
-                t = raw.tile([P, 2048], F32, name="z_raw", tag="raw8", bufs=RAW8)
-                nc.sync.dma_start(out=t[:], in_=z_v[:, a // 4, a % 4, :])
-                tiles[("z", a)] = t
-            elif kind == "Lx":
-                t = raw.tile([P, 4, 1024], BF16, name="x_raw", tag="raw8", bufs=RAW8)
-                nc.sync.dma_start(out=t[:], in_=x_v[:, a, :, :])
-                tiles[("x", a)] = t
-            elif kind == "IW":
-                grp = work.tile([P, 512, 4], BF16, name="grp_w", tag="grp_w", bufs=2, align_bytes=64)
-                tiles[("gw", a)] = grp
-                src = tiles[("w", a)][:].rearrange("p j c -> p c j")
-                if a >= 2 and eng == "V":
-                    nc.vector.tensor_scalar_mul(out=grp[:], in0=src, scalar1=-1.0)
-                elif a >= 2:
-                    nc.scalar.mul(out=grp[:], in_=src, mul=-1.0)
-                else:
-                    copy_on(eng, grp[:], src)
-            elif kind == "QW":
-                nc.vector.quantize_mx(
-                    out=w_codes[:, a, :].bitcast(E4X4), scales=w_scales[:, a, :], in_=flat(tiles[("gw", a)])
-                )
-            elif kind == "IX":
-                grp = work.tile([P, 512, 4], BF16, name="grp_x", tag="grp_w", bufs=2, align_bytes=64)
-                tiles[("gx", a)] = grp
-                src = tiles[("x", a)][:].rearrange("p j (k e) -> p j k e", e=2)[:, :, :, 1].rearrange("p j k -> p k j")
-                copy_on(eng, grp[:], src)
-            elif kind == "QX":
-                nc.vector.quantize_mx(
-                    out=x_codes[:, a, :].bitcast(E4X4), scales=x_scales[:, a, :], in_=flat(tiles[("gx", a)])
-                )
-            elif kind == "D":
-                gr = tiles[("g", a)].rearrange("p (w e) -> p w e", e=2)[:, :, 0]
-                nc.vector.scalar_tensor_tensor(
-                    out=dz_n[a // 4][:, a % 4, :].rearrange("p (h w) -> p h w", h=2),
-                    in0=tiles[("z", a)][:].rearrange("p (h w) -> p h w", h=2),
-                    scalar=0.0,
-                    in1=gr.unsqueeze(1).to_broadcast([P, 2, 1024]),
-                    op0=ALU.is_gt,
-                    op1=ALU.mult,
-                )
-            elif kind == "T":
-                words = dz_n[a // 4][:, a % 4, :].bitcast(F32)
-                tp = psum.tile([P, 512], F32, name="tp", tag="bank")
-                tiles[("tp", a, b)] = tp
-                for gg in range(2):
-                    gp = 2 * b + gg
+        def group_w(f, engine):
+            w_grouped[f] = group(engine, "wx_grouped", 2, w_raw[f][:], negate=(PASS * f >= HALF))
+
+        def quantize_w(f):
+            quantize(w_grouped[f], w_codes[:, f, :], w_scales[:, f, :], E4M3_X4)
+
+        def group_x(g, engine):
+            imaginary = in_raw[g][:].rearrange("p j (k e) -> p j k e", e=2)[:, :, :, 1]
+            x_grouped[g] = group(engine, "wx_grouped", 2, imaginary, negate=False)
+
+        def quantize_x(g):
+            quantize(x_grouped[g], x_codes[:, g, :], x_scales[:, g, :], E4M3_X4)
+
+        def make_s(c):
+            gr = go_raw[c].rearrange("p (f e) -> p f e", e=2)[:, :, 0]
+            nc.vector.scalar_tensor_tensor(
+                out=s_tok[c // PACK][:, c % PACK, :].rearrange("p (h f) -> p h f", h=2),
+                in0=z_raw[c][:].rearrange("p (h f) -> p h f", h=2),
+                scalar=0.0,
+                in1=gr.unsqueeze(1).to_broadcast([P, 2, HALF]),
+                op0=ALU.is_gt,
+                op1=ALU.mult,
+            )
+
+        def transpose_s(c):
+            words = s_tok[c // PACK][:, c % PACK, :].bitcast(F32)
+            for b in range(2):
+                bank = psum.tile([P, BANK], F32, name="dzT_bank", tag="bank")
+                dzT_banks[(c, b)] = bank
+                for i in range(2):
+                    f = 2 * b + i
                     for u in range(2):
                         nc.tensor.transpose(
-                            tp[:, (2 * gg + u) * P : (2 * gg + u + 1) * P],
-                            words[:, 256 * gp + u : 256 * (gp + 1) : 2],
-                            ident[:],
+                            bank[:, (2 * i + u) * P : (2 * i + u + 1) * P],
+                            words[:, 256 * f + u : 256 * (f + 1) : 2],
+                            identity[:],
                         )
-            elif kind == "C":
-                if b == 0:
-                    grp = work.tile([P, 512, 4], BF16, name="grp_b", tag="grp_b", bufs=3, align_bytes=64)
-                    tiles[("gb", a)] = grp
-                grp_w = flat(tiles[("gb", a)]).bitcast(F32)
-                copy_on(
-                    eng,
-                    grp_w[:, 512 * b : 512 * (b + 1)].rearrange("p (s c u) -> p s c u", s=2, u=2),
-                    tiles[("tp", a, b)][:].rearrange("p (s u c) -> p s c u", s=2, u=2),
+
+        def group_sT(c):
+            dzT_grouped[c] = work.tile([P, BANK, PACK], BF16, name="dzT_grouped", tag="dzT_grouped", bufs=3, align_bytes=64)
+            grouped_words = dzT_grouped[c][:].rearrange("p c j -> p (c j)").bitcast(F32)
+            for b in range(2):
+                nc.scalar.copy(
+                    out=grouped_words[:, BANK * b : BANK * (b + 1)].rearrange("p (i t u) -> p i t u", i=2, u=2),
+                    in_=dzT_banks[(c, b)][:].rearrange("p (i u t) -> p i t u", i=2, u=2),
                 )
-            elif kind == "Q":
-                bc = work.tile([P, 512], U32, name="b_codes", tag="b_codes", bufs=3, align_bytes=64)
-                bs = work.tile([P, 512], U8, name="b_scales", tag="b_scales", bufs=3, align_bytes=64)
-                tiles[("bc", a)] = (bc, bs)
-                nc.vector.quantize_mx(out=bc[:].bitcast(E5X4), scales=bs[:], in_=flat(tiles[("gb", a)]))
-            elif kind == "M":
-                bc, bs = tiles[("bc", a)]
-                acc = psum.tile([P, 512], F32, name="acc0", tag="bank")
-                tiles[("acc0", a)] = acc
-                for gp in range(4):
-                    nc.tensor.matmul_mx(
-                        out=acc[:],
-                        lhsT=bc[:, P * gp : P * (gp + 1)].bitcast(E5X4),
-                        lhsT_scale=bs[:, P * gp : P * (gp + 1)],
-                        rhs=w_codes[:, gp, :].bitcast(E4X4),
-                        rhs_scale=w_scales[:, gp, :],
-                        start=(gp == 0),
-                        stop=(gp == 3),
-                    )
-            elif kind == "E":
-                copy_on(eng, st0[a // 2][:, a % 2, :, 1], tiles[("acc0", a)][:])
-            elif kind == "S0":
-                g = a // 2
-                j0 = 2 * (a % 2)
-                nc.sync.dma_start(
-                    out=o0_v[:, g, j0 : j0 + 2, :],
-                    in_=st0[a][:].rearrange("p j k e -> p j (k e)"),
+
+        def quantize_sT(c):
+            codes = work.tile([P, BANK], U32, name="dzT_codes", tag="dzT_codes", bufs=3, align_bytes=64)
+            scales = work.tile([P, BANK], U8, name="dzT_scales", tag="dzT_scales", bufs=3, align_bytes=64)
+            dzT_codes[c] = (codes, scales)
+            quantize(dzT_grouped[c], codes[:], scales[:], E5M2_X4)
+
+        def dx_matmuls(c):
+            codes, scales = dzT_codes[c]
+            dx_bank[c] = psum.tile([P, BANK], F32, name="dx_bank", tag="bank")
+            for f in range(4):
+                nc.tensor.matmul_mx(
+                    out=dx_bank[c][:],
+                    lhsT=codes[:, P * f : P * (f + 1)].bitcast(E5M2_X4),
+                    lhsT_scale=scales[:, P * f : P * (f + 1)],
+                    rhs=w_codes[:, f, :].bitcast(E4M3_X4),
+                    rhs_scale=w_scales[:, f, :],
+                    start=(f == 0),
+                    stop=(f == 3),
                 )
-            elif kind == "I":
-                grp = work.tile([P, 512, 4], BF16, name="grp_a", tag="grp_a", bufs=3, align_bytes=64)
-                tiles[("ga", a, b)] = grp
-                src = dz_n[a][:, :, 512 * b : 512 * (b + 1)].rearrange("p j w -> p w j")
-                if b >= 2:
-                    nc.vector.tensor_scalar_mul(out=grp[:], in0=src, scalar1=-1.0)
-                else:
-                    copy_on(eng, grp[:], src)
-            elif kind == "QA":
-                nc.vector.quantize_mx(
-                    out=a_codes[:, a, 512 * b : 512 * (b + 1)].bitcast(E5X4),
-                    scales=a_scales[:, a, 512 * b : 512 * (b + 1)],
-                    in_=flat(tiles[("ga", a, b)]),
+
+        def evacuate_dx(c):
+            nc.scalar.copy(out=dx_stage[(c // 2) % 2][:, c % 2, :, 1], in_=dx_bank[c][:])
+
+        def store_dx(c):
+            nc.sync.dma_start(
+                out=out_0_view[:, c // PACK, c % PACK : c % PACK + 2, :],
+                in_=dx_stage[(c // 2) % 2][:].rearrange("p i k e -> p i (k e)"),
+            )
+
+        def group_dz(g, f, engine):
+            rows = s_tok[g][:, :, PASS * f : PASS * (f + 1)]
+            dz_grouped[(g, f)] = group(engine, "dz_grouped", 3, rows, negate=(PASS * f >= HALF))
+
+        def quantize_dz(g, f):
+            cols = (PASS * f, PASS * (f + 1))
+            quantize(dz_grouped[(g, f)], dz_codes[:, g, cols[0] : cols[1]], dz_scales[:, g, cols[0] : cols[1]], E5M2_X4)
+
+        def dw_matmuls(t):
+            dw_bank[t] = psum.tile([P, BANK], F32, name="dw_bank", tag="bank")
+            for g in range(2):
+                nc.tensor.matmul_mx(
+                    out=dw_bank[t][:],
+                    lhsT=dz_codes[:, g, P * t : P * (t + 1)].bitcast(E5M2_X4),
+                    lhsT_scale=dz_scales[:, g, P * t : P * (t + 1)],
+                    rhs=x_codes[:, g, :].bitcast(E4M3_X4),
+                    rhs_scale=x_scales[:, g, :],
+                    start=(g == 0),
+                    stop=(g == 1),
                 )
-            elif kind == "MA":
-                acc = psum.tile([P, 512], F32, name="acc1", tag="bank")
-                tiles[("acc1", a)] = acc
-                for g in range(2):
-                    nc.tensor.matmul_mx(
-                        out=acc[:],
-                        lhsT=a_codes[:, g, P * a : P * (a + 1)].bitcast(E5X4),
-                        lhsT_scale=a_scales[:, g, P * a : P * (a + 1)],
-                        rhs=x_codes[:, g, :].bitcast(E4X4),
-                        rhs_scale=x_scales[:, g, :],
-                        start=(g == 0),
-                        stop=(g == 1),
-                    )
-            elif kind == "EA":
-                if ("st1", a // 4) not in tiles:
-                    st = raw.tile([P, 4, 512], F32, name="st1", tag="raw8", bufs=RAW8)
-                    tiles[("st1", a // 4)] = st
-                copy_on(eng, tiles[("st1", a // 4)][:, a % 4, :], tiles[("acc1", a)][:])
-            elif kind == "S1":
-                nc.sync.dma_start(
-                    out=o1_v[:, a : a + b, :], in_=tiles[("st1", a // 4)][:, a % 4 : a % 4 + b, :]
-                )
+
+        def evacuate_dw(t):
+            if t % 4 == 0:
+                dw_stage[t // 4] = loads.tile([P, 4, K_IN], F32, name="dw_stage", tag="big", bufs=BIG_SLOTS)
+            nc.scalar.copy(out=dw_stage[t // 4][:, t % 4, :], in_=dw_bank[t][:])
+
+        def store_dw(t, count):
+            nc.sync.dma_start(
+                out=out_1_view[:, t : t + count, :], in_=dw_stage[t // 4][:, t % 4 : t % 4 + count, :]
+            )
+
+        load_w(0)
+        load_go_tile(0)
+        load_z(0)
+        load_w(1)
+        load_go_tile(1)
+        load_z(1)
+        load_w(2)
+        load_w(3)
+        for c in (2, 4, 6):
+            load_go_pair(c)
+            load_z(c)
+            load_z(c + 1)
+        for i in range(2):
+            for h in range(2):
+                nc.gpsimd.memset(dx_stage[i][:, h, :, :], 0.0)
+
+        group_w(0, "vector")
+        quantize_w(0)
+        make_s(0)
+        load_in(0)
+        transpose_s(0)
+        group_w(1, "scalar")
+        group_sT(0)
+        quantize_w(1)
+        make_s(1)
+        load_in(1)
+        transpose_s(1)
+        group_w(2, "scalar")
+        group_w(3, "vector")
+        group_sT(1)
+        quantize_w(2)
+        quantize_w(3)
+        for c in (0, 1):
+            quantize_sT(c)
+            dx_matmuls(c)
+        evacuate_dx(0)
+        evacuate_dx(1)
+        store_dx(0)
+
+        make_s(2)
+        make_s(3)
+        transpose_s(2)
+        transpose_s(3)
+        group_sT(2)
+        group_sT(3)
+        group_dz(0, 2, "vector")
+        group_dz(0, 0, "scalar")
+        quantize_sT(2)
+        dx_matmuls(2)
+        evacuate_dx(2)
+
+        make_s(4)
+        make_s(5)
+        transpose_s(4)
+        transpose_s(5)
+        group_sT(4)
+        group_dz(0, 1, "scalar")
+        group_sT(5)
+        for c in (3, 4):
+            quantize_sT(c)
+            dx_matmuls(c)
+        evacuate_dx(3)
+        store_dx(2)
+
+        make_s(6)
+        make_s(7)
+        transpose_s(6)
+        transpose_s(7)
+        group_x(0, "scalar")
+        group_sT(6)
+        group_sT(7)
+        quantize_sT(5)
+        dx_matmuls(5)
+        quantize_dz(0, 0)
+        quantize_dz(0, 1)
+        group_x(1, "vector")
+        quantize_x(0)
+        quantize_x(1)
+        for c in (6, 7):
+            quantize_sT(c)
+            dx_matmuls(c)
+        quantize_dz(0, 2)
+        for c in (4, 6):
+            evacuate_dx(c)
+            evacuate_dx(c + 1)
+            store_dx(c)
+
+        pieces = [(1, 0), (1, 1), (1, 2), (1, 3), (0, 3)]
+        group_dz(*pieces[0], "vector")
+        for i in range(1, len(pieces)):
+            group_dz(*pieces[i], "vector")
+            quantize_dz(*pieces[i - 1])
+        quantize_dz(*pieces[-1])
+
+        AHEAD = 3
+        for t in range(16 + AHEAD):
+            if t < 16:
+                dw_matmuls(t)
+            done = t - AHEAD
+            if done >= 0:
+                evacuate_dw(done)
+                if done >= 14:
+                    store_dw(done, 1)
+                elif done % 2 == 1:
+                    store_dw(done - 1, 2)

from contextlib import ExitStack

import concourse.mybir as mybir
from concourse.masks import make_identity

TOKENS, FEATURES, K_IN = 1024, 2048, 512
HALF = FEATURES // 2

FLOPS = 2 * 2 * TOKENS * FEATURES * K_IN
BYTES = 2 * TOKENS * K_IN + 2 * FEATURES * K_IN + 4 * TOKENS * FEATURES + 2 * TOKENS * HALF + 4 * TOKENS * 2 * K_IN + 4 * FEATURES * K_IN

F32 = mybir.dt.float32
BF16 = mybir.dt.bfloat16
U32 = mybir.dt.uint32
U8 = mybir.dt.uint8
E4M3_X4 = mybir.dt.float8_e4m3fn_x4
E5M2_X4 = mybir.dt.float8_e5m2_x4
ALU = mybir.AluOpType

P = 128
PACK = 4
PASS = P * PACK
BANK = 512

BIG_SLOTS = 11
SMALL_SLOTS = 6


def tile_middlelayer_v_kernel(tc, in_data, W, bias, z, grad_out, out_0, out_1):
    nc = tc.nc
    z_view = z.rearrange("(g p j) f -> p g j f", g=2, j=PACK)
    go_view = grad_out.rearrange("(g p j) f o -> p g j (f o)", g=2, j=PACK)
    in_view = in_data.rearrange("(g p j) c -> p g j c", g=2, j=PACK)
    w_view = W.rearrange("(f p j) k -> p f j k", f=4, j=PACK)
    out_0_view = out_0.rearrange("(g p j) c -> p g j c", g=2, j=PACK)
    out_1_view = out_1.rearrange("(t m) k -> m t k", m=P)

    with ExitStack() as ctx:
        loads = ctx.enter_context(tc.tile_pool(name="loads", bufs=1))
        keep = ctx.enter_context(tc.tile_pool(name="keep", bufs=1))
        work = ctx.enter_context(tc.tile_pool(name="work", bufs=1))
        psum = ctx.enter_context(tc.psum_pool(name="psum", bufs=8))
        ctx.enter_context(tc.manual_schedule())

        identity = keep.tile([P, P], F32, name="identity")
        make_identity(nc, identity[:])

        s_tok = []
        for g in range(2):
            s_half = keep.tile([P, PACK, FEATURES], BF16, name="s_tok%d" % g, align_bytes=64)
            s_tok.append(s_half)
        dx_stage = []
        for i in range(2):
            stage = keep.tile([P, 2, K_IN, 2], F32, name="dx_stage%d" % i)
            dx_stage.append(stage)
        w_codes = keep.tile([P, 4, K_IN], U32, name="w_codes", align_bytes=64)
        w_scales = keep.tile([P, 4, K_IN], U8, name="w_scales", align_bytes=64)
        x_codes = keep.tile([P, 2, K_IN], U32, name="x_codes", align_bytes=64)
        x_scales = keep.tile([P, 2, K_IN], U8, name="x_scales", align_bytes=64)
        dz_codes = keep.tile([P, 2, FEATURES], U32, name="dz_codes", align_bytes=64)
        dz_scales = keep.tile([P, 2, FEATURES], U8, name="dz_scales", align_bytes=64)

        w_raw, go_raw, z_raw, in_raw = {}, {}, {}, {}
        w_grouped, x_grouped, dz_grouped, dzT_grouped = {}, {}, {}, {}
        dzT_banks, dzT_codes, dx_bank, dw_bank, dw_stage = {}, {}, {}, {}, {}

        def load_w(f):
            w_raw[f] = loads.tile([P, PACK, K_IN], BF16, name="w_raw", tag="small", bufs=SMALL_SLOTS)
            nc.sync.dma_start(out=w_raw[f][:], in_=w_view[:, f, :, :])

        def load_go_tile(c):
            tile_c = loads.tile([P, FEATURES], BF16, name="go_raw1", tag="small", bufs=SMALL_SLOTS)
            nc.sync.dma_start(out=tile_c[:], in_=go_view[:, c // PACK, c % PACK, :])
            go_raw[c] = tile_c[:]

        def load_go_pair(c):
            pair = loads.tile([P, 2, FEATURES], BF16, name="go_raw2", tag="big", bufs=BIG_SLOTS)
            nc.sync.dma_start(out=pair[:], in_=go_view[:, c // PACK, c % PACK : c % PACK + 2, :])
            go_raw[c] = pair[:, 0, :]
            go_raw[c + 1] = pair[:, 1, :]

        def load_z(c):
            z_raw[c] = loads.tile([P, FEATURES], F32, name="z_raw", tag="big", bufs=BIG_SLOTS)
            nc.sync.dma_start(out=z_raw[c][:], in_=z_view[:, c // PACK, c % PACK, :])

        def load_in(g):
            in_raw[g] = loads.tile([P, PACK, 2 * K_IN], BF16, name="in_raw", tag="big", bufs=BIG_SLOTS)
            nc.sync.dma_start(out=in_raw[g][:], in_=in_view[:, g, :, :])

        def group(engine, tag, bufs, rows, negate):
            grouped = work.tile([P, BANK, PACK], BF16, name=tag, tag=tag, bufs=bufs, align_bytes=64)
            src = rows.rearrange("p j (c i) -> p c j i", i=4)
            dst = grouped[:].rearrange("p (c i) j -> p c j i", i=4)
            if engine == "vector" and negate:
                nc.vector.tensor_scalar_mul(out=dst, in0=src, scalar1=-1.0)
            elif engine == "vector":
                nc.vector.tensor_copy(out=dst, in_=src)
            elif negate:
                nc.scalar.mul(out=dst, in_=src, mul=-1.0)
            else:
                nc.scalar.copy(out=dst, in_=src)
            return grouped

        def quantize(grouped, codes, scales, fmt):
            nc.vector.quantize_mx(
                out=codes.bitcast(fmt), scales=scales, in_=grouped[:].rearrange("p c j -> p (c j)")
            )

        def group_w(f, engine):
            w_grouped[f] = group(engine, "wx_grouped", 2, w_raw[f][:], negate=(PASS * f >= HALF))

        def quantize_w(f):
            quantize(w_grouped[f], w_codes[:, f, :], w_scales[:, f, :], E4M3_X4)

        def group_x(g, engine):
            imaginary = in_raw[g][:].rearrange("p j (k e) -> p j k e", e=2)[:, :, :, 1]
            x_grouped[g] = group(engine, "wx_grouped", 2, imaginary, negate=False)

        def quantize_x(g):
            quantize(x_grouped[g], x_codes[:, g, :], x_scales[:, g, :], E4M3_X4)

        def make_s(c):
            gr = go_raw[c].rearrange("p (f e) -> p f e", e=2)[:, :, 0]
            nc.vector.scalar_tensor_tensor(
                out=s_tok[c // PACK][:, c % PACK, :].rearrange("p (h f) -> p h f", h=2),
                in0=z_raw[c][:].rearrange("p (h f) -> p h f", h=2),
                scalar=0.0,
                in1=gr.unsqueeze(1).to_broadcast([P, 2, HALF]),
                op0=ALU.is_gt,
                op1=ALU.mult,
            )

        def transpose_s(c):
            words = s_tok[c // PACK][:, c % PACK, :].bitcast(F32)
            for b in range(2):
                bank = psum.tile([P, BANK], F32, name="dzT_bank", tag="bank")
                dzT_banks[(c, b)] = bank
                for i in range(2):
                    f = 2 * b + i
                    for u in range(2):
                        nc.tensor.transpose(
                            bank[:, (2 * i + u) * P : (2 * i + u + 1) * P],
                            words[:, 256 * f + u : 256 * (f + 1) : 2],
                            identity[:],
                        )

        def group_sT(c):
            dzT_grouped[c] = work.tile([P, BANK, PACK], BF16, name="dzT_grouped", tag="dzT_grouped", bufs=3, align_bytes=64)
            grouped_words = dzT_grouped[c][:].rearrange("p c j -> p (c j)").bitcast(F32)
            for b in range(2):
                nc.scalar.copy(
                    out=grouped_words[:, BANK * b : BANK * (b + 1)].rearrange("p (i t u) -> p i t u", i=2, u=2),
                    in_=dzT_banks[(c, b)][:].rearrange("p (i u t) -> p i t u", i=2, u=2),
                )

        def quantize_sT(c):
            codes = work.tile([P, BANK], U32, name="dzT_codes", tag="dzT_codes", bufs=3, align_bytes=64)
            scales = work.tile([P, BANK], U8, name="dzT_scales", tag="dzT_scales", bufs=3, align_bytes=64)
            dzT_codes[c] = (codes, scales)
            quantize(dzT_grouped[c], codes[:], scales[:], E5M2_X4)

        def dx_matmuls(c):
            codes, scales = dzT_codes[c]
            dx_bank[c] = psum.tile([P, BANK], F32, name="dx_bank", tag="bank")
            for f in range(4):
                nc.tensor.matmul_mx(
                    out=dx_bank[c][:],
                    lhsT=codes[:, P * f : P * (f + 1)].bitcast(E5M2_X4),
                    lhsT_scale=scales[:, P * f : P * (f + 1)],
                    rhs=w_codes[:, f, :].bitcast(E4M3_X4),
                    rhs_scale=w_scales[:, f, :],
                    start=(f == 0),
                    stop=(f == 3),
                )

        def evacuate_dx(c):
            nc.scalar.copy(out=dx_stage[(c // 2) % 2][:, c % 2, :, 1], in_=dx_bank[c][:])

        def store_dx(c):
            nc.sync.dma_start(
                out=out_0_view[:, c // PACK, c % PACK : c % PACK + 2, :],
                in_=dx_stage[(c // 2) % 2][:].rearrange("p i k e -> p i (k e)"),
            )

        def group_dz(g, f, engine):
            rows = s_tok[g][:, :, PASS * f : PASS * (f + 1)]
            dz_grouped[(g, f)] = group(engine, "dz_grouped", 3, rows, negate=(PASS * f >= HALF))

        def quantize_dz(g, f):
            cols = (PASS * f, PASS * (f + 1))
            quantize(dz_grouped[(g, f)], dz_codes[:, g, cols[0] : cols[1]], dz_scales[:, g, cols[0] : cols[1]], E5M2_X4)

        def dw_matmuls(t):
            dw_bank[t] = psum.tile([P, BANK], F32, name="dw_bank", tag="bank")
            for g in range(2):
                nc.tensor.matmul_mx(
                    out=dw_bank[t][:],
                    lhsT=dz_codes[:, g, P * t : P * (t + 1)].bitcast(E5M2_X4),
                    lhsT_scale=dz_scales[:, g, P * t : P * (t + 1)],
                    rhs=x_codes[:, g, :].bitcast(E4M3_X4),
                    rhs_scale=x_scales[:, g, :],
                    start=(g == 0),
                    stop=(g == 1),
                )

        def evacuate_dw(t):
            if t % 4 == 0:
                dw_stage[t // 4] = loads.tile([P, 4, K_IN], F32, name="dw_stage", tag="big", bufs=BIG_SLOTS)
            nc.scalar.copy(out=dw_stage[t // 4][:, t % 4, :], in_=dw_bank[t][:])

        def store_dw(t, count):
            nc.sync.dma_start(
                out=out_1_view[:, t : t + count, :], in_=dw_stage[t // 4][:, t % 4 : t % 4 + count, :]
            )

        load_w(0)
        load_go_tile(0)
        load_z(0)
        load_w(1)
        load_go_tile(1)
        load_z(1)
        load_w(2)
        load_w(3)
        for c in (2, 4, 6):
            load_go_pair(c)
            load_z(c)
            load_z(c + 1)
        for i in range(2):
            for h in range(2):
                nc.gpsimd.memset(dx_stage[i][:, h, :, :], 0.0)

        group_w(0, "vector")
        quantize_w(0)
        make_s(0)
        load_in(0)
        transpose_s(0)
        group_w(1, "scalar")
        group_sT(0)
        quantize_w(1)
        make_s(1)
        load_in(1)
        transpose_s(1)
        group_w(2, "scalar")
        group_w(3, "vector")
        group_sT(1)
        quantize_w(2)
        quantize_w(3)
        for c in (0, 1):
            quantize_sT(c)
            dx_matmuls(c)
        evacuate_dx(0)
        evacuate_dx(1)
        store_dx(0)

        make_s(2)
        make_s(3)
        transpose_s(2)
        transpose_s(3)
        group_sT(2)
        group_sT(3)
        group_dz(0, 2, "vector")
        group_dz(0, 0, "scalar")
        quantize_sT(2)
        dx_matmuls(2)
        evacuate_dx(2)

        make_s(4)
        make_s(5)
        transpose_s(4)
        transpose_s(5)
        group_sT(4)
        group_dz(0, 1, "scalar")
        group_sT(5)
        for c in (3, 4):
            quantize_sT(c)
            dx_matmuls(c)
        evacuate_dx(3)
        store_dx(2)

        make_s(6)
        make_s(7)
        transpose_s(6)
        transpose_s(7)
        group_x(0, "scalar")
        group_sT(6)
        group_sT(7)
        quantize_sT(5)
        dx_matmuls(5)
        quantize_dz(0, 0)
        quantize_dz(0, 1)
        group_x(1, "vector")
        quantize_x(0)
        quantize_x(1)
        for c in (6, 7):
            quantize_sT(c)
            dx_matmuls(c)
        quantize_dz(0, 2)
        for c in (4, 6):
            evacuate_dx(c)
            evacuate_dx(c + 1)
            store_dx(c)

        pieces = [(1, 0), (1, 1), (1, 2), (1, 3), (0, 3)]
        group_dz(*pieces[0], "vector")
        for i in range(1, len(pieces)):
            group_dz(*pieces[i], "vector")
            quantize_dz(*pieces[i - 1])
        quantize_dz(*pieces[-1])

        AHEAD = 3
        for t in range(16 + AHEAD):
            if t < 16:
                dw_matmuls(t)
            done = t - AHEAD
            if done >= 0:
                evacuate_dw(done)
                if done >= 14:
                    store_dw(done, 1)
                elif done % 2 == 1:
                    store_dw(done - 1, 2)
